import numpy as np
import ml_dtypes


def mxq(x, axis, fmt="e4m3"):
    dtype, down = {"e4m3": (ml_dtypes.float8_e4m3fn, 7), "e5m2": (ml_dtypes.float8_e5m2, 14)}[fmt]
    v = np.moveaxis(np.asarray(x, np.float32).astype(ml_dtypes.bfloat16).astype(np.float64), axis, -1)
    blocks = v.reshape(v.shape[:-1] + (-1, 32))
    amax = np.abs(blocks).max(-1, keepdims=True)
    byte = np.maximum(np.where(amax > 0, np.frexp(amax)[1] - 1 + 127, 0) - down, 1)
    scale = np.exp2(byte - 127.0)
    codes = (blocks / scale).astype(np.float32).astype(dtype).astype(np.float64)
    return np.moveaxis((codes * scale).reshape(v.shape), -1, axis)


WIDE = False


def mx_kscale(k):
    if not WIDE:
        return np.ones(k)
    levels = np.array([10, -10, 5, -5, 0])
    a = np.random.permutation(np.resize(levels, k // 512 * 4)).reshape(k // 512, 4)
    idx = np.arange(k)
    return np.exp2(a[idx // 512, idx % 128 // 32])


BF16 = ml_dtypes.bfloat16


def bf(x):
    return np.asarray(x, np.float32).astype(BF16)


def f64(x):
    return np.asarray(x).astype(np.float64)


B, D, F, A, M = 512, 16384, 512, 32, 512
G = 11.0


def setup_inputs():
    s = mx_kscale(D)
    r = 0.5 + np.random.random_sample((B, 1))
    return {"next_state": bf(np.random.standard_normal((B, D)) * r * s),
            "seen": bf(np.maximum(np.random.standard_normal((M, F)), 0.0) * G / np.sqrt(F)),
            "Wf": bf(np.random.standard_normal((F, D)) * G / np.sqrt(D * F) / s),
            "b_feat": bf(np.random.standard_normal(F) * 0.5 * G / np.sqrt(F))}


def reference(next_state, seen, Wf, b_feat):
    mem = f64(seen)
    fa = np.maximum((mxq(f64(next_state), 1, "e4m3") @ mxq(f64(Wf), 1, "e4m3").T) + f64(b_feat), 0.0)
    a2 = np.sum(fa ** 2, axis=-1, keepdims=True)
    s2 = np.sum(mem ** 2, axis=-1)
    d2 = a2 + s2[None, :] - 2.0 * (mxq(fa, 1, "e4m3") @ mxq(mem, 1, "e4m3").T)
    min_dist = np.sqrt(np.maximum(np.min(d2, axis=-1), 0.0))
    return np.minimum(1.0, min_dist / 10.0)

@@ -1,0 +1,250 @@
+from contextlib import ExitStack
+
+import concourse.mybir as mybir
+from concourse.masks import make_identity
+
+F32 = mybir.dt.float32
+BF16 = mybir.dt.bfloat16
+U32 = mybir.dt.uint32
+U8 = mybir.dt.uint8
+FP8X4 = mybir.dt.float8_e4m3fn_x4
+ACT = mybir.ActivationFunctionType
+ALU = mybir.AluOpType
+AXIS = mybir.AxisListType
+
+P = 128
+PACK = 4
+K_PASS = P * PACK
+ROWS = 512
+ROW_TILES = ROWS // P
+D_STATE = 16384
+D_FEAT = 512
+PASSES = D_STATE // K_PASS
+
+ROUND_PASSES = 2
+SMALL_CHUNK = 2
+BIG_CHUNK = 4
+RAW_BUFS = 3
+
+FLOPS = 2 * ROWS * D_STATE * ROWS + 2 * ROWS * D_FEAT * ROWS
+
+
+def k_onto_partitions(nc, banks, ident, word_block, grouped, vector_takes_last):
+    for half in range(ROW_TILES // 2):
+        bank = banks.tile([P, 2, 2, P], F32, name="bank")
+        for a in range(2):
+            for u in range(2):
+                nc.tensor.transpose(bank[:, a, u, :], word_block(2 * half + a, u), ident[:])
+        bank_read = bank[:].rearrange("p a u r -> p a r u")
+        columns = slice(half * 2 * P * PACK, (half + 1) * 2 * P * PACK)
+        words_out = grouped[:, columns].bitcast(F32).rearrange("p (a r u) -> p a r u", a=2, u=2)
+        if vector_takes_last and half == 1:
+            nc.vector.tensor_copy(out=words_out, in_=bank_read)
+        else:
+            nc.scalar.copy(out=words_out, in_=bank_read)
+
+
+def tile_curiositymodule_pa_k_kernel(tc, next_state, seen, Wf, b_feat, out):
+    nc = tc.nc
+    with ExitStack() as ctx:
+        ctx.enter_context(tc.manual_schedule())
+        const = ctx.enter_context(tc.tile_pool(name="const", bufs=1))
+        raw = ctx.enter_context(tc.tile_pool(name="raw", bufs=RAW_BUFS))
+        stage = ctx.enter_context(tc.tile_pool(name="stage", bufs=3))
+        packed = ctx.enter_context(tc.tile_pool(name="packed", bufs=3))
+        sums = ctx.enter_context(tc.psum_pool(name="sums", bufs=1))
+        banks = ctx.enter_context(tc.psum_pool(name="banks", bufs=4))
+
+        x_rows = next_state.rearrange("(j p) k -> p j k", p=P)
+        w_rows = Wf.rearrange("(p j) k -> p j k", j=ROW_TILES)
+
+        chunk_passes = [SMALL_CHUNK] * 2 + [BIG_CHUNK] * ((PASSES - 2 * SMALL_CHUNK) // BIG_CHUNK)
+        chunk_start = [sum(chunk_passes[:c]) for c in range(len(chunk_passes))]
+
+        def load_chunk(c):
+            k_range = slice(chunk_start[c] * K_PASS, (chunk_start[c] + chunk_passes[c]) * K_PASS)
+            width = chunk_passes[c] * K_PASS
+            x_raw = raw.tile([P, ROW_TILES, BIG_CHUNK * K_PASS], BF16, name="x_raw")
+            nc.sync.dma_start(out=x_raw[:, :, :width], in_=x_rows[:, :, k_range])
+            w_raw = raw.tile([P, ROW_TILES, BIG_CHUNK * K_PASS], BF16, name="w_raw")
+            nc.sync.dma_start(out=w_raw[:, :, :width], in_=w_rows[:, :, k_range])
+            return x_raw, w_raw
+
+        seen_raw = const.tile([P, ROW_TILES, D_FEAT], BF16, name="seen_raw")
+        nc.sync.dma_start(out=seen_raw[:], in_=seen.rearrange("(p j) f -> p j f", j=ROW_TILES))
+        bias_raw = const.tile([P, ROW_TILES], BF16, name="bias_raw")
+        nc.scalar.dma_start(out=bias_raw[:], in_=b_feat.rearrange("(p j) -> p j", j=ROW_TILES))
+        chunks = [load_chunk(c) for c in range(RAW_BUFS)]
+
+        ident = const.tile([P, P], F32, name="ident")
+        make_identity(nc, ident[:])
+        bias = const.tile([P, ROW_TILES], F32, name="bias")
+        nc.gpsimd.tensor_copy(out=bias[:], in_=bias_raw[:])
+
+        one = const.tile([P, 1], F32, name="one")
+        nc.vector.memset(one[:], 1.0)
+        warm = const.tile([P, 1], F32, name="warm")
+        nc.scalar.activation(out=warm[:], in_=one[:], func=ACT.Sqrt)
+        clamped = const.tile([P, P], F32, name="clamped")
+        nc.vector.memset(clamped[:], 0.0)
+
+        seen_grouped = const.tile([P, ROWS * PACK], BF16, name="seen_grouped", align_bytes=64)
+        k_onto_partitions(
+            nc,
+            banks,
+            ident,
+            lambda j, u: seen_raw[:, j, :].bitcast(F32)[:, u : D_FEAT // 2 : 2],
+            seen_grouped,
+            True,
+        )
+        seen_codes = const.tile([P, ROWS], U32, name="seen_codes", align_bytes=64)
+        seen_scales = const.tile([P, ROWS], U8, name="seen_scales", align_bytes=64)
+        nc.vector.quantize_mx(out=seen_codes[:].bitcast(FP8X4), scales=seen_scales[:], in_=seen_grouped[:])
+        seen_sq = const.tile([P, ROW_TILES, D_FEAT], BF16, name="seen_sq")
+        s2 = const.tile([P, ROW_TILES], F32, name="s2")
+        for j in range(ROW_TILES):
+            nc.scalar.activation(
+                out=seen_sq[:, j, :], in_=seen_raw[:, j, :], func=ACT.Square, accum_out=s2[:, j : j + 1]
+            )
+        half_s2 = const.tile([P, ROW_TILES], F32, name="half_s2")
+        nc.vector.tensor_scalar_mul(out=half_s2[:], in0=s2[:], scalar1=0.5)
+
+        fa_sum = [sums.tile([P, ROWS], F32, name="sum%d" % t) for t in range(ROW_TILES)]
+
+        def pack_round(x_raw, w_raw, first_local_pass):
+            x_codes = packed.tile([P, ROUND_PASSES, ROWS], U32, name="x_codes", align_bytes=64)
+            x_scales = packed.tile([P, ROUND_PASSES, ROWS], U8, name="x_scales", align_bytes=64)
+            w_codes = packed.tile([P, ROUND_PASSES, ROWS], U32, name="w_codes", align_bytes=64)
+            w_scales = packed.tile([P, ROUND_PASSES, ROWS], U8, name="w_scales", align_bytes=64)
+            for i in range(ROUND_PASSES):
+                k0 = (first_local_pass + i) * K_PASS
+
+                def block_of(tile_raw):
+                    return lambda j, u: tile_raw[:, j, k0 + 2 * P * u : k0 + 2 * P * (u + 1)].bitcast(F32)
+
+                x_grouped = stage.tile([P, ROWS * PACK], BF16, name="x_grouped", align_bytes=64)
+                k_onto_partitions(nc, banks, ident, block_of(x_raw), x_grouped, False)
+                w_grouped = stage.tile([P, ROWS * PACK], BF16, name="w_grouped", align_bytes=64)
+                k_onto_partitions(nc, banks, ident, block_of(w_raw), w_grouped, True)
+                nc.vector.quantize_mx(
+                    out=x_codes[:, i, :].bitcast(FP8X4), scales=x_scales[:, i, :], in_=x_grouped[:]
+                )
+                nc.vector.quantize_mx(
+                    out=w_codes[:, i, :].bitcast(FP8X4), scales=w_scales[:, i, :], in_=w_grouped[:]
+                )
+            return x_codes, x_scales, w_codes, w_scales
+
+        def multiply_round(first_pass, operands):
+            x_codes, x_scales, w_codes, w_scales = operands
+            for t in range(ROW_TILES):
+                features = slice(t * P, (t + 1) * P)
+                for i in range(ROUND_PASSES):
+                    nc.tensor.matmul_mx(
+                        out=fa_sum[t][:],
+                        lhsT=w_codes[:, i, features].bitcast(FP8X4),
+                        lhsT_scale=w_scales[:, i, features],
+                        rhs=x_codes[:, i, :].bitcast(FP8X4),
+                        rhs_scale=x_scales[:, i, :],
+                        start=(first_pass + i == 0),
+                        stop=(first_pass + i == PASSES - 1),
+                    )
+
+        waiting = None
+        for c in range(len(chunk_passes)):
+            x_raw, w_raw = chunks[c]
+            for local in range(0, chunk_passes[c], ROUND_PASSES):
+                operands = pack_round(x_raw, w_raw, local)
+                if waiting is not None:
+                    multiply_round(waiting[0], waiting[1])
+                waiting = (chunk_start[c] + local, operands)
+            if c + RAW_BUFS < len(chunk_passes):
+                chunks.append(load_chunk(c + RAW_BUFS))
+        multiply_round(waiting[0], waiting[1])
+
+        fa = const.tile([P, ROW_TILES, ROWS], F32, name="fa")
+        fa_by_state = [banks.tile([P, ROW_TILES, P], F32, name="fa_by_state%d" % j, tag="bank") for j in range(ROW_TILES)]
+        for t in range(ROW_TILES):
+            if t % 2 == 0:
+                nc.scalar.activation(
+                    out=fa[:, t, :], in_=fa_sum[t][:], func=ACT.Relu, bias=bias[:, t : t + 1], scale=1.0
+                )
+            else:
+                nc.vector.tensor_scalar(
+                    out=fa[:, t, :],
+                    in0=fa_sum[t][:],
+                    scalar1=bias[:, t : t + 1],
+                    scalar2=0.0,
+                    op0=ALU.add,
+                    op1=ALU.max,
+                )
+            for j in range(ROW_TILES):
+                nc.tensor.transpose(fa_by_state[j][:, t, :], fa[:, t, j * P : (j + 1) * P], ident[:])
+
+        fa_grouped = const.tile([P, ROWS, PACK], BF16, name="fa_grouped", align_bytes=64)
+        for j in range(ROW_TILES):
+            states = slice(j * P, (j + 1) * P)
+            fa_read = fa[:, :, states].rearrange("p t n -> p n t")
+            if j % 2 == 0:
+                nc.vector.tensor_copy(out=fa_grouped[:, states, :], in_=fa_read)
+            else:
+                nc.scalar.copy(out=fa_grouped[:, states, :], in_=fa_read)
+        fa_codes = const.tile([P, ROWS], U32, name="fa_codes", align_bytes=64)
+        fa_scales = const.tile([P, ROWS], U8, name="fa_scales", align_bytes=64)
+        nc.vector.quantize_mx(
+            out=fa_codes[:].bitcast(FP8X4), scales=fa_scales[:], in_=fa_grouped[:].rearrange("p n t -> p (n t)")
+        )
+
+        fa_sq = const.tile([P, ROW_TILES, ROWS], BF16, name="fa_sq")
+        a2 = const.tile([P, ROW_TILES], F32, name="a2")
+        for j in range(ROW_TILES):
+            nc.scalar.activation(
+                out=fa_sq[:, j, :],
+                in_=fa_by_state[j][:].rearrange("p t f -> p (t f)"),
+                func=ACT.Square,
+                accum_out=a2[:, j : j + 1],
+            )
+
+        best = const.tile([P, ROW_TILES, ROWS], F32, name="best")
+        for j in range(ROW_TILES):
+            memory_rows = slice(j * P, (j + 1) * P)
+            cross = sums.tile([P, ROWS], F32, name="cross%d" % j, tag="sum%d" % j)
+            nc.tensor.matmul_mx(
+                out=cross[:],
+                lhsT=seen_codes[:, memory_rows].bitcast(FP8X4),
+                lhsT_scale=seen_scales[:, memory_rows],
+                rhs=fa_codes[:].bitcast(FP8X4),
+                rhs_scale=fa_scales[:],
+                start=True,
+                stop=True,
+            )
+            if j == 0:
+                nc.vector.tensor_scalar(
+                    out=best[:, j, :], in0=cross[:], scalar1=half_s2[:, j : j + 1], scalar2=None, op0=ALU.subtract
+                )
+            else:
+                nc.vector.scalar_tensor_tensor(
+                    out=best[:, j, :],
+                    in0=cross[:],
+                    scalar=half_s2[:, j : j + 1],
+                    in1=best[:, j - 1, :],
+                    op0=ALU.subtract,
+                    op1=ALU.max,
+                )
+        best_by_state = banks.tile([P, ROW_TILES, P], F32, name="best_by_state", tag="bank")
+        for j in range(ROW_TILES):
+            nc.tensor.transpose(best_by_state[:, j, :], best[:, ROW_TILES - 1, j * P : (j + 1) * P], ident[:])
+        best_max = const.tile([P, ROW_TILES], F32, name="best_max")
+        nc.vector.tensor_reduce(out=best_max[:], in_=best_by_state[:], axis=AXIS.X, op=ALU.max)
+
+        d2 = const.tile([P, ROW_TILES], F32, name="d2")
+        nc.vector.scalar_tensor_tensor(
+            out=d2[:], in0=best_max[:], scalar=-2.0, in1=a2[:], op0=ALU.mult, op1=ALU.add
+        )
+        nc.vector.tensor_scalar(
+            out=clamped[:, :ROW_TILES], in0=d2[:], scalar1=0.0, scalar2=100.0, op0=ALU.max, op1=ALU.min
+        )
+        clamped_rows = banks.tile([P, P], F32, name="clamped_rows", tag="bank")
+        nc.tensor.transpose(clamped_rows[:], clamped[:], ident[:])
+        novelty = const.tile([P, P], F32, name="novelty")
+        nc.scalar.activation(out=novelty[:], in_=clamped_rows[:], func=ACT.Sqrt, scale=0.01)
+        nc.sync.dma_start(out=out.rearrange("(j p) -> j p", p=P), in_=novelty[:ROW_TILES, :])

@@ -21,7 +21,7 @@ D_STATE = 16384
 D_FEAT = 512
 PASSES = D_STATE // K_PASS
 
-ROUND_PASSES = 2
+ROUND_PASSES = 1
 SMALL_CHUNK = 2
 BIG_CHUNK = 4
 RAW_BUFS = 3

@@ -22,6 +22,7 @@ D_FEAT = 512
 PASSES = D_STATE // K_PASS
 
 ROUND_PASSES = 1
+LAG = 2
 SMALL_CHUNK = 2
 BIG_CHUNK = 4
 RAW_BUFS = 3
@@ -51,7 +52,7 @@ def tile_curiositymodule_pa_k_kernel(tc, next_state, seen, Wf, b_feat, out):
         const = ctx.enter_context(tc.tile_pool(name="const", bufs=1))
         raw = ctx.enter_context(tc.tile_pool(name="raw", bufs=RAW_BUFS))
         stage = ctx.enter_context(tc.tile_pool(name="stage", bufs=3))
-        packed = ctx.enter_context(tc.tile_pool(name="packed", bufs=3))
+        packed = ctx.enter_context(tc.tile_pool(name="packed", bufs=LAG + 2))
         sums = ctx.enter_context(tc.psum_pool(name="sums", bufs=1))
         banks = ctx.enter_context(tc.psum_pool(name="banks", bufs=4))
 
@@ -149,17 +150,17 @@ def tile_curiositymodule_pa_k_kernel(tc, next_state, seen, Wf, b_feat, out):
                         stop=(first_pass + i == PASSES - 1),
                     )
 
-        waiting = None
+        rounds = []
         for c in range(len(chunk_passes)):
             x_raw, w_raw = chunks[c]
             for local in range(0, chunk_passes[c], ROUND_PASSES):
-                operands = pack_round(x_raw, w_raw, local)
-                if waiting is not None:
-                    multiply_round(waiting[0], waiting[1])
-                waiting = (chunk_start[c] + local, operands)
+                rounds.append((chunk_start[c] + local, pack_round(x_raw, w_raw, local)))
+                if len(rounds) > LAG:
+                    multiply_round(*rounds[len(rounds) - 1 - LAG])
             if c + RAW_BUFS < len(chunk_passes):
                 chunks.append(load_chunk(c + RAW_BUFS))
-        multiply_round(waiting[0], waiting[1])
+        for late in rounds[len(rounds) - LAG :]:
+            multiply_round(*late)
 
         fa = const.tile([P, ROW_TILES, ROWS], F32, name="fa")
         fa_by_state = [banks.tile([P, ROW_TILES, P], F32, name="fa_by_state%d" % j, tag="bank") for j in range(ROW_TILES)]

@@ -19,19 +19,20 @@ ROWS = 512
 ROW_TILES = ROWS // P
 D_STATE = 16384
 D_FEAT = 512
-PASSES = D_STATE // K_PASS
 
-ROUND_PASSES = 1
-LAG = 2
-SMALL_CHUNK = 2
-BIG_CHUNK = 4
-RAW_BUFS = 3
+TILE_PASSES = 4
+TILE_K = TILE_PASSES * K_PASS
+CHUNKS = D_STATE // TILE_K
+TILES = CHUNKS * ROW_TILES
+HEAD_TILES = ROW_TILES + 1
+FIRST_LOADS = 12
+RAW_BUFS = FIRST_LOADS // 2 + 1
 
 FLOPS = 2 * ROWS * D_STATE * ROWS + 2 * ROWS * D_FEAT * ROWS
 
 
-def k_onto_partitions(nc, banks, ident, word_block, grouped, vector_takes_last):
-    for half in range(ROW_TILES // 2):
+def k_onto_partitions(nc, banks, ident, word_block, grouped, vector_takes_first):
+    for half in range(2):
         bank = banks.tile([P, 2, 2, P], F32, name="bank")
         for a in range(2):
             for u in range(2):
@@ -39,7 +40,7 @@ def k_onto_partitions(nc, banks, ident, word_block, grouped, vector_takes_last):
         bank_read = bank[:].rearrange("p a u r -> p a r u")
         columns = slice(half * 2 * P * PACK, (half + 1) * 2 * P * PACK)
         words_out = grouped[:, columns].bitcast(F32).rearrange("p (a r u) -> p a r u", a=2, u=2)
-        if vector_takes_last and half == 1:
+        if vector_takes_first and half == 0:
             nc.vector.tensor_copy(out=words_out, in_=bank_read)
         else:
             nc.scalar.copy(out=words_out, in_=bank_read)
@@ -51,31 +52,46 @@ def tile_curiositymodule_pa_k_kernel(tc, next_state, seen, Wf, b_feat, out):
         ctx.enter_context(tc.manual_schedule())
         const = ctx.enter_context(tc.tile_pool(name="const", bufs=1))
         raw = ctx.enter_context(tc.tile_pool(name="raw", bufs=RAW_BUFS))
-        stage = ctx.enter_context(tc.tile_pool(name="stage", bufs=3))
-        packed = ctx.enter_context(tc.tile_pool(name="packed", bufs=LAG + 2))
+        stage = ctx.enter_context(tc.tile_pool(name="stage", bufs=4))
+        w_packed = ctx.enter_context(tc.tile_pool(name="w_packed", bufs=4))
+        x_packed = ctx.enter_context(tc.tile_pool(name="x_packed", bufs=3))
         sums = ctx.enter_context(tc.psum_pool(name="sums", bufs=1))
         banks = ctx.enter_context(tc.psum_pool(name="banks", bufs=4))
 
-        x_rows = next_state.rearrange("(j p) k -> p j k", p=P)
-        w_rows = Wf.rearrange("(p j) k -> p j k", j=ROW_TILES)
+        x_rows = next_state.rearrange("(j p) k -> j p k", p=P)
+        w_rows = Wf.rearrange("(p t) k -> t p k", t=ROW_TILES)
+        seen_rows = seen.rearrange("(p j) f -> p (j f)", j=ROW_TILES)
 
-        chunk_passes = [SMALL_CHUNK] * 2 + [BIG_CHUNK] * ((PASSES - 2 * SMALL_CHUNK) // BIG_CHUNK)
-        chunk_start = [sum(chunk_passes[:c]) for c in range(len(chunk_passes))]
+        order = [("x", i) for i in range(ROW_TILES)] + [("w", 0)]
+        for r in range(TILES):
+            if r + 1 < TILES:
+                order.append(("w", r + 1))
+            if r + ROW_TILES < TILES:
+                order.append(("x", r + ROW_TILES))
+        order.append(("seen", 0))
+        raw_tiles = []
 
-        def load_chunk(c):
-            k_range = slice(chunk_start[c] * K_PASS, (chunk_start[c] + chunk_passes[c]) * K_PASS)
-            width = chunk_passes[c] * K_PASS
-            x_raw = raw.tile([P, ROW_TILES, BIG_CHUNK * K_PASS], BF16, name="x_raw")
-            nc.sync.dma_start(out=x_raw[:, :, :width], in_=x_rows[:, :, k_range])
-            w_raw = raw.tile([P, ROW_TILES, BIG_CHUNK * K_PASS], BF16, name="w_raw")
-            nc.sync.dma_start(out=w_raw[:, :, :width], in_=w_rows[:, :, k_range])
-            return x_raw, w_raw
+        def load(n):
+            kind, i = order[n]
+            chunk, row_tile = divmod(i, ROW_TILES)
+            k_range = slice(chunk * TILE_K, (chunk + 1) * TILE_K)
+            if kind == "x":
+                x_raw = raw.tile([P, TILE_K], BF16, name="x_raw")
+                nc.sync.dma_start(out=x_raw[:], in_=x_rows[row_tile, :, k_range])
+                raw_tiles.append(x_raw)
+            elif kind == "w":
+                w_raw = raw.tile([P, TILE_K], BF16, name="w_raw")
+                nc.sync.dma_start(out=w_raw[:], in_=w_rows[row_tile, :, k_range])
+                raw_tiles.append(w_raw)
+            else:
+                seen_raw = const.tile([P, ROW_TILES * D_FEAT], BF16, name="seen_raw")
+                nc.sync.dma_start(out=seen_raw[:], in_=seen_rows)
+                raw_tiles.append(seen_raw)
 
-        seen_raw = const.tile([P, ROW_TILES, D_FEAT], BF16, name="seen_raw")
-        nc.sync.dma_start(out=seen_raw[:], in_=seen.rearrange("(p j) f -> p j f", j=ROW_TILES))
+        for n in range(FIRST_LOADS):
+            load(n)
         bias_raw = const.tile([P, ROW_TILES], BF16, name="bias_raw")
-        nc.scalar.dma_start(out=bias_raw[:], in_=b_feat.rearrange("(p j) -> p j", j=ROW_TILES))
-        chunks = [load_chunk(c) for c in range(RAW_BUFS)]
+        nc.scalar.dma_start(out=bias_raw[:], in_=b_feat.rearrange("(p t) -> p t", t=ROW_TILES))
 
         ident = const.tile([P, P], F32, name="ident")
         make_identity(nc, ident[:])
@@ -89,112 +105,109 @@ def tile_curiositymodule_pa_k_kernel(tc, next_state, seen, Wf, b_feat, out):
         clamped = const.tile([P, P], F32, name="clamped")
         nc.vector.memset(clamped[:], 0.0)
 
-        seen_grouped = const.tile([P, ROWS * PACK], BF16, name="seen_grouped", align_bytes=64)
-        k_onto_partitions(
-            nc,
-            banks,
-            ident,
-            lambda j, u: seen_raw[:, j, :].bitcast(F32)[:, u : D_FEAT // 2 : 2],
-            seen_grouped,
-            True,
-        )
+        x_codes = {}
+        x_scales = {}
+        w_codes = {}
+        w_scales = {}
         seen_codes = const.tile([P, ROWS], U32, name="seen_codes", align_bytes=64)
         seen_scales = const.tile([P, ROWS], U8, name="seen_scales", align_bytes=64)
-        nc.vector.quantize_mx(out=seen_codes[:].bitcast(FP8X4), scales=seen_scales[:], in_=seen_grouped[:])
-        seen_sq = const.tile([P, ROW_TILES, D_FEAT], BF16, name="seen_sq")
-        s2 = const.tile([P, ROW_TILES], F32, name="s2")
-        for j in range(ROW_TILES):
-            nc.scalar.activation(
-                out=seen_sq[:, j, :], in_=seen_raw[:, j, :], func=ACT.Square, accum_out=s2[:, j : j + 1]
-            )
-        half_s2 = const.tile([P, ROW_TILES], F32, name="half_s2")
-        nc.vector.tensor_scalar_mul(out=half_s2[:], in0=s2[:], scalar1=0.5)
+
+        def pack(n):
+            kind, i = order[n]
+            chunk, row_tile = divmod(i, ROW_TILES)
+            tile_raw = raw_tiles[n]
+            grouped = stage.tile([P, TILE_PASSES * P * PACK], BF16, name="grouped", align_bytes=64)
+            vector_takes_first = n % 2 == 1
+            if kind == "seen":
+                def word_block(a, u):
+                    return tile_raw[:, a * D_FEAT : (a + 1) * D_FEAT].bitcast(F32)[:, u : D_FEAT // 2 : 2]
+
+            else:
+                def word_block(a, u):
+                    first = a * K_PASS + u * 2 * P
+                    return tile_raw[:, first : first + 2 * P].bitcast(F32)
+
+            k_onto_partitions(nc, banks, ident, word_block, grouped, vector_takes_first)
+            if kind == "seen":
+                nc.vector.quantize_mx(out=seen_codes[:].bitcast(FP8X4), scales=seen_scales[:], in_=grouped[:])
+            elif kind == "w":
+                w_codes[i] = w_packed.tile([P, TILE_PASSES * P], U32, name="w_codes", align_bytes=64)
+                w_scales[i] = w_packed.tile([P, TILE_PASSES * P], U8, name="w_scales", align_bytes=64)
+                nc.vector.quantize_mx(out=w_codes[i][:].bitcast(FP8X4), scales=w_scales[i][:], in_=grouped[:])
+            else:
+                if row_tile == 0:
+                    x_codes[chunk] = x_packed.tile([P, TILE_PASSES, ROWS], U32, name="x_codes", align_bytes=64)
+                    x_scales[chunk] = x_packed.tile([P, TILE_PASSES, ROWS], U8, name="x_scales", align_bytes=64)
+                states = slice(row_tile * P, (row_tile + 1) * P)
+                for g in range(TILE_PASSES):
+                    nc.vector.quantize_mx(
+                        out=x_codes[chunk][:, g, states].bitcast(FP8X4),
+                        scales=x_scales[chunk][:, g, states],
+                        in_=grouped[:, g * P * PACK : (g + 1) * P * PACK],
+                    )
+            if n + FIRST_LOADS < len(order):
+                load(n + FIRST_LOADS)
 
         fa_sum = [sums.tile([P, ROWS], F32, name="sum%d" % t) for t in range(ROW_TILES)]
 
-        def pack_round(x_raw, w_raw, first_local_pass):
-            x_codes = packed.tile([P, ROUND_PASSES, ROWS], U32, name="x_codes", align_bytes=64)
-            x_scales = packed.tile([P, ROUND_PASSES, ROWS], U8, name="x_scales", align_bytes=64)
-            w_codes = packed.tile([P, ROUND_PASSES, ROWS], U32, name="w_codes", align_bytes=64)
-            w_scales = packed.tile([P, ROUND_PASSES, ROWS], U8, name="w_scales", align_bytes=64)
-            for i in range(ROUND_PASSES):
-                k0 = (first_local_pass + i) * K_PASS
-
-                def block_of(tile_raw):
-                    return lambda j, u: tile_raw[:, j, k0 + 2 * P * u : k0 + 2 * P * (u + 1)].bitcast(F32)
-
-                x_grouped = stage.tile([P, ROWS * PACK], BF16, name="x_grouped", align_bytes=64)
-                k_onto_partitions(nc, banks, ident, block_of(x_raw), x_grouped, False)
-                w_grouped = stage.tile([P, ROWS * PACK], BF16, name="w_grouped", align_bytes=64)
-                k_onto_partitions(nc, banks, ident, block_of(w_raw), w_grouped, True)
-                nc.vector.quantize_mx(
-                    out=x_codes[:, i, :].bitcast(FP8X4), scales=x_scales[:, i, :], in_=x_grouped[:]
+        def multiply(r):
+            chunk, t = divmod(r, ROW_TILES)
+            for g in range(TILE_PASSES):
+                features = slice(g * P, (g + 1) * P)
+                nc.tensor.matmul_mx(
+                    out=fa_sum[t][:],
+                    lhsT=w_codes[r][:, features].bitcast(FP8X4),
+                    lhsT_scale=w_scales[r][:, features],
+                    rhs=x_codes[chunk][:, g, :].bitcast(FP8X4),
+                    rhs_scale=x_scales[chunk][:, g, :],
+                    start=(chunk == 0 and g == 0),
+                    stop=(chunk == CHUNKS - 1 and g == TILE_PASSES - 1),
                 )
-                nc.vector.quantize_mx(
-                    out=w_codes[:, i, :].bitcast(FP8X4), scales=w_scales[:, i, :], in_=w_grouped[:]
-                )
-            return x_codes, x_scales, w_codes, w_scales
-
-        def multiply_round(first_pass, operands):
-            x_codes, x_scales, w_codes, w_scales = operands
-            for t in range(ROW_TILES):
-                features = slice(t * P, (t + 1) * P)
-                for i in range(ROUND_PASSES):
-                    nc.tensor.matmul_mx(
-                        out=fa_sum[t][:],
-                        lhsT=w_codes[:, i, features].bitcast(FP8X4),
-                        lhsT_scale=w_scales[:, i, features],
-                        rhs=x_codes[:, i, :].bitcast(FP8X4),
-                        rhs_scale=x_scales[:, i, :],
-                        start=(first_pass + i == 0),
-                        stop=(first_pass + i == PASSES - 1),
-                    )
-
-        rounds = []
-        for c in range(len(chunk_passes)):
-            x_raw, w_raw = chunks[c]
-            for local in range(0, chunk_passes[c], ROUND_PASSES):
-                rounds.append((chunk_start[c] + local, pack_round(x_raw, w_raw, local)))
-                if len(rounds) > LAG:
-                    multiply_round(*rounds[len(rounds) - 1 - LAG])
-            if c + RAW_BUFS < len(chunk_passes):
-                chunks.append(load_chunk(c + RAW_BUFS))
-        for late in rounds[len(rounds) - LAG :]:
-            multiply_round(*late)
 
         fa = const.tile([P, ROW_TILES, ROWS], F32, name="fa")
-        fa_by_state = [banks.tile([P, ROW_TILES, P], F32, name="fa_by_state%d" % j, tag="bank") for j in range(ROW_TILES)]
-        for t in range(ROW_TILES):
-            if t % 2 == 0:
-                nc.scalar.activation(
-                    out=fa[:, t, :], in_=fa_sum[t][:], func=ACT.Relu, bias=bias[:, t : t + 1], scale=1.0
-                )
-            else:
-                nc.vector.tensor_scalar(
-                    out=fa[:, t, :],
-                    in0=fa_sum[t][:],
-                    scalar1=bias[:, t : t + 1],
-                    scalar2=0.0,
-                    op0=ALU.add,
-                    op1=ALU.max,
-                )
-            for j in range(ROW_TILES):
-                nc.tensor.transpose(fa_by_state[j][:, t, :], fa[:, t, j * P : (j + 1) * P], ident[:])
-
         fa_grouped = const.tile([P, ROWS, PACK], BF16, name="fa_grouped", align_bytes=64)
-        for j in range(ROW_TILES):
-            states = slice(j * P, (j + 1) * P)
-            fa_read = fa[:, :, states].rearrange("p t n -> p n t")
-            if j % 2 == 0:
-                nc.vector.tensor_copy(out=fa_grouped[:, states, :], in_=fa_read)
-            else:
-                nc.scalar.copy(out=fa_grouped[:, states, :], in_=fa_read)
+
+        def finish_features(t):
+            nc.scalar.activation(
+                out=fa[:, t, :], in_=fa_sum[t][:], func=ACT.Relu, bias=bias[:, t : t + 1], scale=1.0
+            )
+            nc.vector.tensor_copy(out=fa_grouped[:, :, t], in_=fa[:, t, :])
+
+        seen_sq = const.tile([P, ROW_TILES, D_FEAT], BF16, name="seen_sq")
+        s2 = const.tile([P, ROW_TILES], F32, name="s2")
+        seen_round = (len(order) - 1 - HEAD_TILES) // 2
+
+        for n in range(HEAD_TILES):
+            pack(n)
+        for r in range(TILES):
+            for n in range(HEAD_TILES + 2 * r, min(HEAD_TILES + 2 * r + 2, len(order))):
+                pack(n)
+            if seen_round - ROW_TILES <= r < seen_round:
+                j = r - (seen_round - ROW_TILES)
+                nc.scalar.activation(
+                    out=seen_sq[:, j, :],
+                    in_=raw_tiles[len(order) - 1][:, j * D_FEAT : (j + 1) * D_FEAT],
+                    func=ACT.Square,
+                    accum_out=s2[:, j : j + 1],
+                )
+            multiply(r)
+            if r >= TILES - ROW_TILES:
+                finish_features(r % ROW_TILES)
+
+        half_s2 = const.tile([P, ROW_TILES], F32, name="half_s2")
+        nc.vector.tensor_scalar_mul(out=half_s2[:], in0=s2[:], scalar1=0.5)
         fa_codes = const.tile([P, ROWS], U32, name="fa_codes", align_bytes=64)
         fa_scales = const.tile([P, ROWS], U8, name="fa_scales", align_bytes=64)
         nc.vector.quantize_mx(
             out=fa_codes[:].bitcast(FP8X4), scales=fa_scales[:], in_=fa_grouped[:].rearrange("p n t -> p (n t)")
         )
 
+        fa_by_state = [
+            banks.tile([P, ROW_TILES, P], F32, name="fa_by_state%d" % j, tag="bank") for j in range(ROW_TILES)
+        ]
+        for t in range(ROW_TILES):
+            for j in range(ROW_TILES):
+                nc.tensor.transpose(fa_by_state[j][:, t, :], fa[:, t, j * P : (j + 1) * P], ident[:])
         fa_sq = const.tile([P, ROW_TILES, ROWS], BF16, name="fa_sq")
         a2 = const.tile([P, ROW_TILES], F32, name="a2")
         for j in range(ROW_TILES):

@@ -24,6 +24,8 @@ TILE_PASSES = 4
 TILE_K = TILE_PASSES * K_PASS
 CHUNKS = D_STATE // TILE_K
 TILES = CHUNKS * ROW_TILES
+HALVES = 2
+HALF = ROWS // HALVES
 HEAD_TILES = ROW_TILES + 1
 FIRST_LOADS = 12
 RAW_BUFS = FIRST_LOADS // 2 + 1
@@ -166,12 +168,14 @@ def tile_curiositymodule_pa_k_kernel(tc, next_state, seen, Wf, b_feat, out):
 
         fa = const.tile([P, ROW_TILES, ROWS], F32, name="fa")
         fa_grouped = const.tile([P, ROWS, PACK], BF16, name="fa_grouped", align_bytes=64)
+        everyone = slice(0, ROWS)
+        halves = [slice(h * HALF, (h + 1) * HALF) for h in range(HALVES)]
 
-        def finish_features(t):
+        def finish_features(t, states):
             nc.scalar.activation(
-                out=fa[:, t, :], in_=fa_sum[t][:], func=ACT.Relu, bias=bias[:, t : t + 1], scale=1.0
+                out=fa[:, t, states], in_=fa_sum[t][:, states], func=ACT.Relu, bias=bias[:, t : t + 1], scale=1.0
             )
-            nc.vector.tensor_copy(out=fa_grouped[:, :, t], in_=fa[:, t, :])
+            nc.vector.tensor_copy(out=fa_grouped[:, states, t], in_=fa[:, t, states])
 
         seen_sq = const.tile([P, ROW_TILES, D_FEAT], BF16, name="seen_sq")
         s2 = const.tile([P, ROW_TILES], F32, name="s2")
@@ -191,26 +195,33 @@ def tile_curiositymodule_pa_k_kernel(tc, next_state, seen, Wf, b_feat, out):
                     accum_out=s2[:, j : j + 1],
                 )
             multiply(r)
-            if r >= TILES - ROW_TILES:
-                finish_features(r % ROW_TILES)
+            if TILES - ROW_TILES <= r < TILES - 1:
+                finish_features(r % ROW_TILES, everyone)
 
-        half_s2 = const.tile([P, ROW_TILES], F32, name="half_s2")
-        nc.vector.tensor_scalar_mul(out=half_s2[:], in0=s2[:], scalar1=0.5)
+        minus_half_s2 = const.tile([P, ROW_TILES], F32, name="minus_half_s2")
+        nc.vector.tensor_scalar_mul(out=minus_half_s2[:], in0=s2[:], scalar1=-0.5)
+        for states in halves:
+            finish_features(ROW_TILES - 1, states)
+
         fa_codes = const.tile([P, ROWS], U32, name="fa_codes", align_bytes=64)
         fa_scales = const.tile([P, ROWS], U8, name="fa_scales", align_bytes=64)
-        nc.vector.quantize_mx(
-            out=fa_codes[:].bitcast(FP8X4), scales=fa_scales[:], in_=fa_grouped[:].rearrange("p n t -> p (n t)")
-        )
+        for states in halves:
+            nc.vector.quantize_mx(
+                out=fa_codes[:, states].bitcast(FP8X4),
+                scales=fa_scales[:, states],
+                in_=fa_grouped[:, states, :].rearrange("p n t -> p (n t)"),
+            )
 
-        fa_by_state = [
-            banks.tile([P, ROW_TILES, P], F32, name="fa_by_state%d" % j, tag="bank") for j in range(ROW_TILES)
-        ]
-        for t in range(ROW_TILES):
-            for j in range(ROW_TILES):
-                nc.tensor.transpose(fa_by_state[j][:, t, :], fa[:, t, j * P : (j + 1) * P], ident[:])
+        fa_by_state = []
+        for j in range(ROW_TILES):
+            by_state = banks.tile([P, ROW_TILES, P], F32, name="by_state", tag="bank")
+            for t in range(ROW_TILES):
+                nc.tensor.transpose(by_state[:, t, :], fa[:, t, j * P : (j + 1) * P], ident[:])
+            fa_by_state.append(by_state)
         fa_sq = const.tile([P, ROW_TILES, ROWS], BF16, name="fa_sq")
         a2 = const.tile([P, ROW_TILES], F32, name="a2")
-        for j in range(ROW_TILES):
+
+        def square_features(j):
             nc.scalar.activation(
                 out=fa_sq[:, j, :],
                 in_=fa_by_state[j][:].rearrange("p t f -> p (t f)"),
@@ -218,37 +229,60 @@ def tile_curiositymodule_pa_k_kernel(tc, next_state, seen, Wf, b_feat, out):
                 accum_out=a2[:, j : j + 1],
             )
 
-        best = const.tile([P, ROW_TILES, ROWS], F32, name="best")
-        for j in range(ROW_TILES):
-            memory_rows = slice(j * P, (j + 1) * P)
-            cross = sums.tile([P, ROWS], F32, name="cross%d" % j, tag="sum%d" % j)
-            nc.tensor.matmul_mx(
-                out=cross[:],
-                lhsT=seen_codes[:, memory_rows].bitcast(FP8X4),
-                lhsT_scale=seen_scales[:, memory_rows],
-                rhs=fa_codes[:].bitcast(FP8X4),
-                rhs_scale=fa_scales[:],
-                start=True,
-                stop=True,
-            )
-            if j == 0:
-                nc.vector.tensor_scalar(
-                    out=best[:, j, :], in0=cross[:], scalar1=half_s2[:, j : j + 1], scalar2=None, op0=ALU.subtract
+        square_features(0)
+        square_features(1)
+
+        odd = {}
+        even = {}
+        best = {}
+        for h, states in enumerate(halves):
+            odd[h] = sums.tile([P, 2, HALF], F32, name="odd%d" % h, tag="sum%d" % (2 * h))
+            even[h] = sums.tile([P, 2, HALF], F32, name="even%d" % h, tag="sum%d" % (2 * h + 1))
+            for cross, j in ((odd[h], 1), (odd[h], 3), (even[h], 0), (even[h], 2)):
+                memory_rows = slice(j * P, (j + 1) * P)
+                nc.tensor.matmul_mx(
+                    out=cross[:, j // 2, :],
+                    lhsT=seen_codes[:, memory_rows].bitcast(FP8X4),
+                    lhsT_scale=seen_scales[:, memory_rows],
+                    rhs=fa_codes[:, states].bitcast(FP8X4),
+                    rhs_scale=fa_scales[:, states],
+                    start=True,
+                    stop=True,
                 )
-            else:
+            best[h] = const.tile([P, 2, HALF], F32, name="best%d" % h)
+            for e in range(2):
+                other = const.tile([P, HALF], F32, name="other%d%d" % (h, e))
+                nc.scalar.activation(
+                    out=other[:],
+                    in_=odd[h][:, e, :],
+                    func=ACT.Identity,
+                    bias=minus_half_s2[:, 2 * e + 1 : 2 * e + 2],
+                    scale=1.0,
+                )
                 nc.vector.scalar_tensor_tensor(
-                    out=best[:, j, :],
-                    in0=cross[:],
-                    scalar=half_s2[:, j : j + 1],
-                    in1=best[:, j - 1, :],
-                    op0=ALU.subtract,
+                    out=best[h][:, e, :],
+                    in0=even[h][:, e, :],
+                    scalar=minus_half_s2[:, 2 * e : 2 * e + 1],
+                    in1=other[:],
+                    op0=ALU.add,
                     op1=ALU.max,
                 )
-        best_by_state = banks.tile([P, ROW_TILES, P], F32, name="best_by_state", tag="bank")
-        for j in range(ROW_TILES):
-            nc.tensor.transpose(best_by_state[:, j, :], best[:, ROW_TILES - 1, j * P : (j + 1) * P], ident[:])
+        square_features(2)
+        square_features(3)
+
         best_max = const.tile([P, ROW_TILES], F32, name="best_max")
-        nc.vector.tensor_reduce(out=best_max[:], in_=best_by_state[:], axis=AXIS.X, op=ALU.max)
+        half_tiles = ROW_TILES // HALVES
+        for h in range(HALVES):
+            best_by_state = sums.tile([P, half_tiles, 2, P], F32, name="best_by_state%d" % h, tag="sum%d" % (2 * h))
+            for e in range(2):
+                for j in range(half_tiles):
+                    nc.tensor.transpose(best_by_state[:, j, e, :], best[h][:, e, j * P : (j + 1) * P], ident[:])
+            nc.vector.tensor_reduce(
+                out=best_max[:, h * half_tiles : (h + 1) * half_tiles],
+                in_=best_by_state[:].rearrange("p j e r -> p j (e r)"),
+                axis=AXIS.X,
+                op=ALU.max,
+            )
 
         d2 = const.tile([P, ROW_TILES], F32, name="d2")
         nc.vector.scalar_tensor_tensor(
@@ -257,7 +291,7 @@ def tile_curiositymodule_pa_k_kernel(tc, next_state, seen, Wf, b_feat, out):
         nc.vector.tensor_scalar(
             out=clamped[:, :ROW_TILES], in0=d2[:], scalar1=0.0, scalar2=100.0, op0=ALU.max, op1=ALU.min
         )
-        clamped_rows = banks.tile([P, P], F32, name="clamped_rows", tag="bank")
+        clamped_rows = sums.tile([P, P], F32, name="clamped_rows", tag="sum1")
         nc.tensor.transpose(clamped_rows[:], clamped[:], ident[:])
         novelty = const.tile([P, P], F32, name="novelty")
         nc.scalar.activation(out=novelty[:], in_=clamped_rows[:], func=ACT.Sqrt, scale=0.01)

@@ -27,6 +27,7 @@ TILES = CHUNKS * ROW_TILES
 HALVES = 2
 HALF = ROWS // HALVES
 HEAD_TILES = ROW_TILES + 1
+SEEN_LOAD = 32
 FIRST_LOADS = 12
 RAW_BUFS = FIRST_LOADS // 2 + 1
 
@@ -72,6 +73,7 @@ def tile_curiositymodule_pa_k_kernel(tc, next_state, seen, Wf, b_feat, out):
                 order.append(("x", r + ROW_TILES))
         order.append(("seen", 0))
         raw_tiles = []
+        seen_tiles = []
 
         def load(n):
             kind, i = order[n]
@@ -88,7 +90,7 @@ def tile_curiositymodule_pa_k_kernel(tc, next_state, seen, Wf, b_feat, out):
             else:
                 seen_raw = const.tile([P, ROW_TILES * D_FEAT], BF16, name="seen_raw")
                 nc.sync.dma_start(out=seen_raw[:], in_=seen_rows)
-                raw_tiles.append(seen_raw)
+                seen_tiles.append(seen_raw)
 
         for n in range(FIRST_LOADS):
             load(n)
@@ -117,7 +119,7 @@ def tile_curiositymodule_pa_k_kernel(tc, next_state, seen, Wf, b_feat, out):
         def pack(n):
             kind, i = order[n]
             chunk, row_tile = divmod(i, ROW_TILES)
-            tile_raw = raw_tiles[n]
+            tile_raw = seen_tiles[0] if kind == "seen" else raw_tiles[n]
             grouped = stage.tile([P, TILE_PASSES * P * PACK], BF16, name="grouped", align_bytes=64)
             vector_takes_first = n % 2 == 1
             if kind == "seen":
@@ -147,8 +149,10 @@ def tile_curiositymodule_pa_k_kernel(tc, next_state, seen, Wf, b_feat, out):
                         scales=x_scales[chunk][:, g, states],
                         in_=grouped[:, g * P * PACK : (g + 1) * P * PACK],
                     )
-            if n + FIRST_LOADS < len(order):
+            if n + FIRST_LOADS < len(order) - 1:
                 load(n + FIRST_LOADS)
+            if n == SEEN_LOAD:
+                load(len(order) - 1)
 
         fa_sum = [sums.tile([P, ROWS], F32, name="sum%d" % t) for t in range(ROW_TILES)]
 
@@ -190,7 +194,7 @@ def tile_curiositymodule_pa_k_kernel(tc, next_state, seen, Wf, b_feat, out):
                 j = r - (seen_round - ROW_TILES)
                 nc.scalar.activation(
                     out=seen_sq[:, j, :],
-                    in_=raw_tiles[len(order) - 1][:, j * D_FEAT : (j + 1) * D_FEAT],
+                    in_=seen_tiles[0][:, j * D_FEAT : (j + 1) * D_FEAT],
                     func=ACT.Square,
                     accum_out=s2[:, j : j + 1],
                 )

@@ -26,6 +26,8 @@ CHUNKS = D_STATE // TILE_K
 TILES = CHUNKS * ROW_TILES
 HALVES = 2
 HALF = ROWS // HALVES
+WARM_START = 6
+WARM_TILE = 2
 HEAD_TILES = ROW_TILES + 1
 SEEN_LOAD = 32
 FIRST_LOADS = 12
@@ -106,6 +108,8 @@ def tile_curiositymodule_pa_k_kernel(tc, next_state, seen, Wf, b_feat, out):
         nc.vector.memset(one[:], 1.0)
         warm = const.tile([P, 1], F32, name="warm")
         nc.scalar.activation(out=warm[:], in_=one[:], func=ACT.Sqrt)
+        zeros = const.tile([P, ROWS], BF16, name="zeros")
+        nc.vector.memset(zeros[:], 0.0)
         clamped = const.tile([P, P], F32, name="clamped")
         nc.vector.memset(clamped[:], 0.0)
 
@@ -185,8 +189,14 @@ def tile_curiositymodule_pa_k_kernel(tc, next_state, seen, Wf, b_feat, out):
         s2 = const.tile([P, ROW_TILES], F32, name="s2")
         seen_round = (len(order) - 1 - HEAD_TILES) // 2
 
+        def keep_warm(times):
+            for i in range(times):
+                nc.tensor.matmul(out=fa_sum[ROW_TILES - 1][:], lhsT=zeros[:, :P], rhs=zeros[:], start=True, stop=True)
+
+        keep_warm(WARM_START)
         for n in range(HEAD_TILES):
             pack(n)
+            keep_warm(WARM_TILE)
         for r in range(TILES):
             for n in range(HEAD_TILES + 2 * r, min(HEAD_TILES + 2 * r + 2, len(order))):
                 pack(n)

from contextlib import ExitStack

import concourse.mybir as mybir
from concourse.masks import make_identity

F32 = mybir.dt.float32
BF16 = mybir.dt.bfloat16
U32 = mybir.dt.uint32
U8 = mybir.dt.uint8
FP8X4 = mybir.dt.float8_e4m3fn_x4
ACT = mybir.ActivationFunctionType
ALU = mybir.AluOpType
AXIS = mybir.AxisListType

P = 128
PACK = 4
K_PASS = P * PACK
ROWS = 512
ROW_TILES = ROWS // P
D_STATE = 16384
D_FEAT = 512

TILE_PASSES = 4
TILE_K = TILE_PASSES * K_PASS
CHUNKS = D_STATE // TILE_K
TILES = CHUNKS * ROW_TILES
HALVES = 2
HALF = ROWS // HALVES
WARM_START = 6
WARM_TILE = 2
HEAD_TILES = ROW_TILES + 1
SEEN_LOAD = 32
FIRST_LOADS = 12
RAW_BUFS = FIRST_LOADS // 2 + 1

FLOPS = 2 * ROWS * D_STATE * ROWS + 2 * ROWS * D_FEAT * ROWS


def k_onto_partitions(nc, banks, ident, word_block, grouped, vector_takes_first):
    for half in range(2):
        bank = banks.tile([P, 2, 2, P], F32, name="bank")
        for a in range(2):
            for u in range(2):
                nc.tensor.transpose(bank[:, a, u, :], word_block(2 * half + a, u), ident[:])
        bank_read = bank[:].rearrange("p a u r -> p a r u")
        columns = slice(half * 2 * P * PACK, (half + 1) * 2 * P * PACK)
        words_out = grouped[:, columns].bitcast(F32).rearrange("p (a r u) -> p a r u", a=2, u=2)
        if vector_takes_first and half == 0:
            nc.vector.tensor_copy(out=words_out, in_=bank_read)
        else:
            nc.scalar.copy(out=words_out, in_=bank_read)


def tile_curiositymodule_pa_k_kernel(tc, next_state, seen, Wf, b_feat, out):
    nc = tc.nc
    with ExitStack() as ctx:
        ctx.enter_context(tc.manual_schedule())
        const = ctx.enter_context(tc.tile_pool(name="const", bufs=1))
        raw = ctx.enter_context(tc.tile_pool(name="raw", bufs=RAW_BUFS))
        stage = ctx.enter_context(tc.tile_pool(name="stage", bufs=4))
        w_packed = ctx.enter_context(tc.tile_pool(name="w_packed", bufs=4))
        x_packed = ctx.enter_context(tc.tile_pool(name="x_packed", bufs=3))
        sums = ctx.enter_context(tc.psum_pool(name="sums", bufs=1))
        banks = ctx.enter_context(tc.psum_pool(name="banks", bufs=4))

        x_rows = next_state.rearrange("(j p) k -> j p k", p=P)
        w_rows = Wf.rearrange("(p t) k -> t p k", t=ROW_TILES)
        seen_rows = seen.rearrange("(p j) f -> p (j f)", j=ROW_TILES)

        order = [("x", i) for i in range(ROW_TILES)] + [("w", 0)]
        for r in range(TILES):
            if r + 1 < TILES:
                order.append(("w", r + 1))
            if r + ROW_TILES < TILES:
                order.append(("x", r + ROW_TILES))
        order.append(("seen", 0))
        raw_tiles = []
        seen_tiles = []

        def load(n):
            kind, i = order[n]
            chunk, row_tile = divmod(i, ROW_TILES)
            k_range = slice(chunk * TILE_K, (chunk + 1) * TILE_K)
            if kind == "x":
                x_raw = raw.tile([P, TILE_K], BF16, name="x_raw")
                nc.sync.dma_start(out=x_raw[:], in_=x_rows[row_tile, :, k_range])
                raw_tiles.append(x_raw)
            elif kind == "w":
                w_raw = raw.tile([P, TILE_K], BF16, name="w_raw")
                nc.sync.dma_start(out=w_raw[:], in_=w_rows[row_tile, :, k_range])
                raw_tiles.append(w_raw)
            else:
                seen_raw = const.tile([P, ROW_TILES * D_FEAT], BF16, name="seen_raw")
                nc.sync.dma_start(out=seen_raw[:], in_=seen_rows)
                seen_tiles.append(seen_raw)

        for n in range(FIRST_LOADS):
            load(n)
        bias_raw = const.tile([P, ROW_TILES], BF16, name="bias_raw")
        nc.scalar.dma_start(out=bias_raw[:], in_=b_feat.rearrange("(p t) -> p t", t=ROW_TILES))

        ident = const.tile([P, P], F32, name="ident")
        make_identity(nc, ident[:])
        bias = const.tile([P, ROW_TILES], F32, name="bias")
        nc.gpsimd.tensor_copy(out=bias[:], in_=bias_raw[:])

        one = const.tile([P, 1], F32, name="one")
        nc.vector.memset(one[:], 1.0)
        warm = const.tile([P, 1], F32, name="warm")
        nc.scalar.activation(out=warm[:], in_=one[:], func=ACT.Sqrt)
        zeros = const.tile([P, ROWS], BF16, name="zeros")
        nc.vector.memset(zeros[:], 0.0)
        clamped = const.tile([P, P], F32, name="clamped")
        nc.vector.memset(clamped[:], 0.0)

        x_codes = {}
        x_scales = {}
        w_codes = {}
        w_scales = {}
        seen_codes = const.tile([P, ROWS], U32, name="seen_codes", align_bytes=64)
        seen_scales = const.tile([P, ROWS], U8, name="seen_scales", align_bytes=64)

        def pack(n):
            kind, i = order[n]
            chunk, row_tile = divmod(i, ROW_TILES)
            tile_raw = seen_tiles[0] if kind == "seen" else raw_tiles[n]
            grouped = stage.tile([P, TILE_PASSES * P * PACK], BF16, name="grouped", align_bytes=64)
            vector_takes_first = n % 2 == 1
            if kind == "seen":
                def word_block(a, u):
                    return tile_raw[:, a * D_FEAT : (a + 1) * D_FEAT].bitcast(F32)[:, u : D_FEAT // 2 : 2]

            else:
                def word_block(a, u):
                    first = a * K_PASS + u * 2 * P
                    return tile_raw[:, first : first + 2 * P].bitcast(F32)

            k_onto_partitions(nc, banks, ident, word_block, grouped, vector_takes_first)
            if kind == "seen":
                nc.vector.quantize_mx(out=seen_codes[:].bitcast(FP8X4), scales=seen_scales[:], in_=grouped[:])
            elif kind == "w":
                w_codes[i] = w_packed.tile([P, TILE_PASSES * P], U32, name="w_codes", align_bytes=64)
                w_scales[i] = w_packed.tile([P, TILE_PASSES * P], U8, name="w_scales", align_bytes=64)
                nc.vector.quantize_mx(out=w_codes[i][:].bitcast(FP8X4), scales=w_scales[i][:], in_=grouped[:])
            else:
                if row_tile == 0:
                    x_codes[chunk] = x_packed.tile([P, TILE_PASSES, ROWS], U32, name="x_codes", align_bytes=64)
                    x_scales[chunk] = x_packed.tile([P, TILE_PASSES, ROWS], U8, name="x_scales", align_bytes=64)
                states = slice(row_tile * P, (row_tile + 1) * P)
                for g in range(TILE_PASSES):
                    nc.vector.quantize_mx(
                        out=x_codes[chunk][:, g, states].bitcast(FP8X4),
                        scales=x_scales[chunk][:, g, states],
                        in_=grouped[:, g * P * PACK : (g + 1) * P * PACK],
                    )
            if n + FIRST_LOADS < len(order) - 1:
                load(n + FIRST_LOADS)
            if n == SEEN_LOAD:
                load(len(order) - 1)

        fa_sum = [sums.tile([P, ROWS], F32, name="sum%d" % t) for t in range(ROW_TILES)]

        def multiply(r):
            chunk, t = divmod(r, ROW_TILES)
            for g in range(TILE_PASSES):
                features = slice(g * P, (g + 1) * P)
                nc.tensor.matmul_mx(
                    out=fa_sum[t][:],
                    lhsT=w_codes[r][:, features].bitcast(FP8X4),
                    lhsT_scale=w_scales[r][:, features],
                    rhs=x_codes[chunk][:, g, :].bitcast(FP8X4),
                    rhs_scale=x_scales[chunk][:, g, :],
                    start=(chunk == 0 and g == 0),
                    stop=(chunk == CHUNKS - 1 and g == TILE_PASSES - 1),
                )

        fa = const.tile([P, ROW_TILES, ROWS], F32, name="fa")
        fa_grouped = const.tile([P, ROWS, PACK], BF16, name="fa_grouped", align_bytes=64)
        everyone = slice(0, ROWS)
        halves = [slice(h * HALF, (h + 1) * HALF) for h in range(HALVES)]

        def finish_features(t, states):
            nc.scalar.activation(
                out=fa[:, t, states], in_=fa_sum[t][:, states], func=ACT.Relu, bias=bias[:, t : t + 1], scale=1.0
            )
            nc.vector.tensor_copy(out=fa_grouped[:, states, t], in_=fa[:, t, states])

        seen_sq = const.tile([P, ROW_TILES, D_FEAT], BF16, name="seen_sq")
        s2 = const.tile([P, ROW_TILES], F32, name="s2")
        seen_round = (len(order) - 1 - HEAD_TILES) // 2

        def keep_warm(times):
            for i in range(times):
                nc.tensor.matmul(out=fa_sum[ROW_TILES - 1][:], lhsT=zeros[:, :P], rhs=zeros[:], start=True, stop=True)

        keep_warm(WARM_START)
        for n in range(HEAD_TILES):
            pack(n)
            keep_warm(WARM_TILE)
        for r in range(TILES):
            for n in range(HEAD_TILES + 2 * r, min(HEAD_TILES + 2 * r + 2, len(order))):
                pack(n)
            if seen_round - ROW_TILES <= r < seen_round:
                j = r - (seen_round - ROW_TILES)
                nc.scalar.activation(
                    out=seen_sq[:, j, :],
                    in_=seen_tiles[0][:, j * D_FEAT : (j + 1) * D_FEAT],
                    func=ACT.Square,
                    accum_out=s2[:, j : j + 1],
                )
            multiply(r)
            if TILES - ROW_TILES <= r < TILES - 1:
                finish_features(r % ROW_TILES, everyone)

        minus_half_s2 = const.tile([P, ROW_TILES], F32, name="minus_half_s2")
        nc.vector.tensor_scalar_mul(out=minus_half_s2[:], in0=s2[:], scalar1=-0.5)
        for states in halves:
            finish_features(ROW_TILES - 1, states)

        fa_codes = const.tile([P, ROWS], U32, name="fa_codes", align_bytes=64)
        fa_scales = const.tile([P, ROWS], U8, name="fa_scales", align_bytes=64)
        for states in halves:
            nc.vector.quantize_mx(
                out=fa_codes[:, states].bitcast(FP8X4),
                scales=fa_scales[:, states],
                in_=fa_grouped[:, states, :].rearrange("p n t -> p (n t)"),
            )

        fa_by_state = []
        for j in range(ROW_TILES):
            by_state = banks.tile([P, ROW_TILES, P], F32, name="by_state", tag="bank")
            for t in range(ROW_TILES):
                nc.tensor.transpose(by_state[:, t, :], fa[:, t, j * P : (j + 1) * P], ident[:])
            fa_by_state.append(by_state)
        fa_sq = const.tile([P, ROW_TILES, ROWS], BF16, name="fa_sq")
        a2 = const.tile([P, ROW_TILES], F32, name="a2")

        def square_features(j):
            nc.scalar.activation(
                out=fa_sq[:, j, :],
                in_=fa_by_state[j][:].rearrange("p t f -> p (t f)"),
                func=ACT.Square,
                accum_out=a2[:, j : j + 1],
            )

        square_features(0)
        square_features(1)

        odd = {}
        even = {}
        best = {}
        for h, states in enumerate(halves):
            odd[h] = sums.tile([P, 2, HALF], F32, name="odd%d" % h, tag="sum%d" % (2 * h))
            even[h] = sums.tile([P, 2, HALF], F32, name="even%d" % h, tag="sum%d" % (2 * h + 1))
            for cross, j in ((odd[h], 1), (odd[h], 3), (even[h], 0), (even[h], 2)):
                memory_rows = slice(j * P, (j + 1) * P)
                nc.tensor.matmul_mx(
                    out=cross[:, j // 2, :],
                    lhsT=seen_codes[:, memory_rows].bitcast(FP8X4),
                    lhsT_scale=seen_scales[:, memory_rows],
                    rhs=fa_codes[:, states].bitcast(FP8X4),
                    rhs_scale=fa_scales[:, states],
                    start=True,
                    stop=True,
                )
            best[h] = const.tile([P, 2, HALF], F32, name="best%d" % h)
            for e in range(2):
                other = const.tile([P, HALF], F32, name="other%d%d" % (h, e))
                nc.scalar.activation(
                    out=other[:],
                    in_=odd[h][:, e, :],
                    func=ACT.Identity,
                    bias=minus_half_s2[:, 2 * e + 1 : 2 * e + 2],
                    scale=1.0,
                )
                nc.vector.scalar_tensor_tensor(
                    out=best[h][:, e, :],
                    in0=even[h][:, e, :],
                    scalar=minus_half_s2[:, 2 * e : 2 * e + 1],
                    in1=other[:],
                    op0=ALU.add,
                    op1=ALU.max,
                )
        square_features(2)
        square_features(3)

        best_max = const.tile([P, ROW_TILES], F32, name="best_max")
        half_tiles = ROW_TILES // HALVES
        for h in range(HALVES):
            best_by_state = sums.tile([P, half_tiles, 2, P], F32, name="best_by_state%d" % h, tag="sum%d" % (2 * h))
            for e in range(2):
                for j in range(half_tiles):
                    nc.tensor.transpose(best_by_state[:, j, e, :], best[h][:, e, j * P : (j + 1) * P], ident[:])
            nc.vector.tensor_reduce(
                out=best_max[:, h * half_tiles : (h + 1) * half_tiles],
                in_=best_by_state[:].rearrange("p j e r -> p j (e r)"),
                axis=AXIS.X,
                op=ALU.max,
            )

        d2 = const.tile([P, ROW_TILES], F32, name="d2")
        nc.vector.scalar_tensor_tensor(
            out=d2[:], in0=best_max[:], scalar=-2.0, in1=a2[:], op0=ALU.mult, op1=ALU.add
        )
        nc.vector.tensor_scalar(
            out=clamped[:, :ROW_TILES], in0=d2[:], scalar1=0.0, scalar2=100.0, op0=ALU.max, op1=ALU.min
        )
        clamped_rows = sums.tile([P, P], F32, name="clamped_rows", tag="sum1")
        nc.tensor.transpose(clamped_rows[:], clamped[:], ident[:])
        novelty = const.tile([P, P], F32, name="novelty")
        nc.scalar.activation(out=novelty[:], in_=clamped_rows[:], func=ACT.Sqrt, scale=0.01)
        nc.sync.dma_start(out=out.rearrange("(j p) -> j p", p=P), in_=novelty[:ROW_TILES, :])
